import numpy as np
import ml_dtypes


def mxq(x, axis, fmt="e4m3"):
    dtype, down = {"e4m3": (ml_dtypes.float8_e4m3fn, 7), "e5m2": (ml_dtypes.float8_e5m2, 14)}[fmt]
    v = np.moveaxis(np.asarray(x, np.float32).astype(ml_dtypes.bfloat16).astype(np.float64), axis, -1)
    blocks = v.reshape(v.shape[:-1] + (-1, 32))
    amax = np.abs(blocks).max(-1, keepdims=True)
    byte = np.maximum(np.where(amax > 0, np.frexp(amax)[1] - 1 + 127, 0) - down, 1)
    scale = np.exp2(byte - 127.0)
    codes = (blocks / scale).astype(np.float32).astype(dtype).astype(np.float64)
    return np.moveaxis((codes * scale).reshape(v.shape), -1, axis)


WIDE = False


def mx_kscale(k):
    if not WIDE:
        return np.ones(k)
    levels = np.array([10, -10, 5, -5, 0])
    if k % 512:
        return np.exp2(np.random.permutation(np.resize(levels, k // 32))).repeat(32)
    a = np.empty((k // 512, 16))
    for p in range(k // 512):
        a[p, :8] = np.random.permutation(np.resize(levels, 8))
        for g in range(8):
            far = levels[np.abs(levels - a[p, g]) >= 10]
            a[p, g + 8] = far[np.random.randint(len(far))]
    return np.exp2(a.ravel()).repeat(32)


BF16 = ml_dtypes.bfloat16


def bf(x):
    return np.asarray(x, np.float32).astype(BF16)


def f64(x):
    return np.asarray(x).astype(np.float64)


B, S, DIM, H, NOPE, ROPE_SP, V_SP, KV_RANK = 8, 1024, 1024, 2, 64, 64, 128, 512
C = 1.0
QK_SP = NOPE + ROPE_SP


def lift(sp):
    return np.concatenate([np.sqrt((sp * sp).sum(-1, keepdims=True) + C), sp], -1)


def rope(u, cos, sin):
    u1, u2 = u[..., 0::2], u[..., 1::2]
    cos, sin = cos[None, :, None, :], sin[None, :, None, :]
    return np.stack([u1 * cos - u2 * sin, u1 * sin + u2 * cos], -1).reshape(u.shape)


def setup_inputs():
    s = mx_kscale(DIM)
    inv = 1.0 / (10000.0 ** (np.arange(0, ROPE_SP, 2) / ROPE_SP))
    ang = np.arange(S)[:, None] * inv[None, :]
    return {"x": bf(np.random.standard_normal((B, S, DIM)) * s),
            "freqs_cos": bf(np.cos(ang)),
            "freqs_sin": bf(np.sin(ang)),
            "wq_w": bf(np.random.standard_normal((H * QK_SP, DIM)) * 0.3 / np.sqrt(DIM) / s[None, :]),
            "wq_b": bf(np.random.standard_normal(H * QK_SP) * 0.1)}


def reference(x, freqs_cos, freqs_sin, wq_w, wq_b):
    q = (mxq(f64(x), 2, "e4m3") @ mxq(f64(wq_w), 1, "e4m3").T) + f64(wq_b)
    q = q.reshape(B, S, H, QK_SP)
    q_nope, q_pe = q[..., :NOPE], q[..., NOPE:]
    q_pe = rope(q_pe, f64(freqs_cos), f64(freqs_sin))
    return lift(np.concatenate([q_nope, q_pe], -1))

@@ -1,0 +1,259 @@
+from contextlib import ExitStack
+
+import concourse.mybir as mybir
+from concourse.masks import make_identity
+
+F32 = mybir.dt.float32
+BF16 = mybir.dt.bfloat16
+U32 = mybir.dt.uint32
+U8 = mybir.dt.uint8
+FP8X4 = mybir.dt.float8_e4m3fn_x4
+ACT = mybir.ActivationFunctionType
+ALU = mybir.AluOpType
+
+P = 128
+BATCH, SEQ, K = 8, 1024, 1024
+HEADS, HEAD, NOPE, PAIRS = 2, 128, 64, 32
+FEATURES = HEADS * HEAD
+ROW = HEAD + 1
+TOKENS_PER_PARTITION = SEQ // P
+PASSES = K // 512
+WORDS = K // 2
+GROUP_TILES = 2
+CHUNK_TILES = 4
+GROUPS_PER_CHUNK = CHUNK_TILES // GROUP_TILES
+CHUNKS_PER_BATCH = TOKENS_PER_PARTITION // CHUNK_TILES
+N_CHUNKS = BATCH * CHUNKS_PER_BATCH
+N_GROUPS = N_CHUNKS * GROUPS_PER_CHUNK
+GROUP_ROWS = GROUP_TILES * HEADS
+CHUNK_ROWS = CHUNK_TILES * HEADS
+
+FLOPS = 2 * BATCH * SEQ * K * FEATURES
+
+
+def tile_lorentzmla_pb_t_kernel(tc, x, freqs_cos, freqs_sin, wq_w, wq_b, out):
+    nc = tc.nc
+    with ExitStack() as stack:
+        const = stack.enter_context(tc.tile_pool(name="const", bufs=1))
+        x_pool = stack.enter_context(tc.tile_pool(name="x", bufs=N_CHUNKS))
+        grouped_pool = stack.enter_context(tc.tile_pool(name="grouped", bufs=3))
+        mx_pool = stack.enter_context(tc.tile_pool(name="mx", bufs=3))
+        rope_pool = stack.enter_context(tc.tile_pool(name="rope", bufs=3))
+        out_pool = stack.enter_context(tc.tile_pool(name="out", bufs=6))
+        turned_pool = stack.enter_context(tc.psum_pool(name="turned", bufs=4))
+        acc_pool = stack.enter_context(tc.psum_pool(name="acc", bufs=4))
+        stack.enter_context(tc.manual_schedule())
+
+        w_sb = const.tile([P, HEADS * K], BF16)
+        w_dst = w_sb[:].rearrange("f (h k) -> f h k", h=HEADS)
+        w_src = wq_w.rearrange("(h f) k -> f h k", h=HEADS)
+        w_rotary = w_src[NOPE:HEAD].rearrange("(j e) h k -> e j h k", e=2)
+        nc.scalar.dma_start(out=w_dst[0:NOPE], in_=w_src[0:NOPE])
+        nc.scalar.dma_start(out=w_dst[NOPE : NOPE + PAIRS], in_=w_rotary[0])
+        nc.scalar.dma_start(out=w_dst[NOPE + PAIRS : HEAD], in_=w_rotary[1])
+
+        x_src = x.rearrange("b (p i) k -> b p (i k)", i=TOKENS_PER_PARTITION)
+        x_chunks = []
+
+        def load_chunk(c):
+            b, part = divmod(c, CHUNKS_PER_BATCH)
+            x_sb = x_pool.tile([P, CHUNK_TILES * K], BF16)
+            cols = slice(part * CHUNK_TILES * K, (part + 1) * CHUNK_TILES * K)
+            nc.sync.dma_start(out=x_sb[:], in_=x_src[b][:, cols])
+            x_chunks.append(x_sb)
+
+        load_chunk(0)
+        cos_sb = const.tile([P, TOKENS_PER_PARTITION * PAIRS], BF16)
+        sin_sb = const.tile([P, TOKENS_PER_PARTITION * PAIRS], BF16)
+        bias_bf = const.tile([P, FEATURES], BF16)
+        nc.scalar.dma_start(out=cos_sb[:], in_=freqs_cos.rearrange("(p i) j -> p (i j)", i=TOKENS_PER_PARTITION))
+        nc.scalar.dma_start(out=sin_sb[:], in_=freqs_sin.rearrange("(p i) j -> p (i j)", i=TOKENS_PER_PARTITION))
+        nc.scalar.dma_start(out=bias_bf[:], in_=wq_b.partition_broadcast(P))
+        for c in range(1, N_CHUNKS):
+            load_chunk(c)
+
+        ident = const.tile([P, P], F32)
+        make_identity(nc, ident[:])
+
+        warm = const.tile([P, 1], F32)
+        nc.vector.memset(warm[:], 1.0)
+        nc.scalar.sqrt(out=warm[:], in_=warm[:])
+
+        def transpose_rows(rows_bf16):
+            words = rows_bf16.bitcast(F32)
+            turned = turned_pool.tile([P, WORDS], F32)
+            for block in range(WORDS // P):
+                g, u = divmod(block, 2)
+                nc.tensor.transpose(
+                    turned[:, block * P : (block + 1) * P], words[:, 2 * P * g + u : 2 * P * (g + 1) : 2], ident[:]
+                )
+            return turned
+
+        def regroup(copy, turned, grouped, t):
+            dst = grouped[:].bitcast(F32).rearrange("p (g t r u) -> p g t r u", g=PASSES, t=GROUP_TILES, u=2)
+            copy(out=dst[:, :, t], in_=turned[:].rearrange("p (g u r) -> p g r u", g=PASSES, u=2))
+
+        def quantise(grouped, codes, scales):
+            nc.vector.quantize_mx(out=codes[:].bitcast(FP8X4), scales=scales[:], in_=grouped[:])
+
+        w_grouped = const.tile([P, GROUP_TILES * K], BF16, align_bytes=64)
+        w_codes = const.tile([P, PASSES * FEATURES], U32, align_bytes=64)
+        w_scales = const.tile([P, PASSES * FEATURES], U8, align_bytes=64)
+        for h in range(HEADS):
+            w_turned = transpose_rows(w_sb[:, h * K : (h + 1) * K])
+            regroup(nc.vector.tensor_copy, w_turned, w_grouped, h)
+        quantise(w_grouped, w_codes, w_scales)
+
+        sin_neg = const.tile([P, TOKENS_PER_PARTITION * PAIRS], BF16)
+        nc.vector.tensor_scalar_mul(out=sin_neg[:], in0=sin_sb[:], scalar1=-1.0)
+        bias = const.tile([P, FEATURES], F32)
+        bias_src = bias_bf[:].rearrange("p (h f) -> p h f", h=HEADS)
+        bias_dst = bias[:].rearrange("p (h f) -> p h f", h=HEADS)
+        nc.vector.tensor_copy(out=bias_dst[:, :, 0:NOPE], in_=bias_src[:, :, 0:NOPE])
+        nc.vector.tensor_copy(
+            out=bias_dst[:, :, NOPE:HEAD].rearrange("p h (e j) -> p h e j", e=2),
+            in_=bias_src[:, :, NOPE:HEAD].rearrange("p h (j e) -> p h e j", e=2),
+        )
+        bias_rows = bias[:].rearrange("p (o h f) -> p o h f", o=1, h=HEADS).to_broadcast([P, GROUP_TILES, HEADS, HEAD])
+
+        def angles(table, n, repeat):
+            i0 = (n * GROUP_TILES) % TOKENS_PER_PARTITION
+            view = table[:].rearrange("p (i o j) -> p i o j", o=1, j=PAIRS)[:, i0 : i0 + GROUP_TILES]
+            return view.to_broadcast([P, GROUP_TILES, repeat, PAIRS])
+
+        turned_of, grouped_of, mx_of, acc_of, rope_of, out_of, squares_of = {}, {}, {}, {}, {}, {}, {}
+
+        def transpose_group(n):
+            c, part = divmod(n, GROUPS_PER_CHUNK)
+            first = part * GROUP_TILES
+            turned_of[n] = [
+                transpose_rows(x_chunks[c][:, (first + t) * K : (first + t + 1) * K]) for t in range(GROUP_TILES)
+            ]
+
+        def regroup_group(n):
+            grouped = grouped_pool.tile([P, GROUP_TILES * K], BF16, align_bytes=64)
+            for t in range(GROUP_TILES):
+                regroup(nc.scalar.copy, turned_of[n][t], grouped, t)
+            grouped_of[n] = grouped
+
+        def quantise_group(n):
+            codes = mx_pool.tile([P, PASSES * GROUP_TILES * P], U32, align_bytes=64)
+            scales = mx_pool.tile([P, PASSES * GROUP_TILES * P], U8, align_bytes=64)
+            quantise(grouped_of[n], codes, scales)
+            mx_of[n] = (codes, scales)
+
+        def multiply_group(n):
+            codes, scales = mx_of[n]
+            acc = acc_pool.tile([P, GROUP_TILES * FEATURES], F32)
+            for t in range(GROUP_TILES):
+                for g in range(PASSES):
+                    tokens = slice((g * GROUP_TILES + t) * P, (g * GROUP_TILES + t + 1) * P)
+                    feats = slice(g * FEATURES, (g + 1) * FEATURES)
+                    nc.tensor.matmul_mx(
+                        out=acc[:, t * FEATURES : (t + 1) * FEATURES],
+                        lhsT=codes[:, tokens].bitcast(FP8X4),
+                        lhsT_scale=scales[:, tokens],
+                        rhs=w_codes[:, feats].bitcast(FP8X4),
+                        rhs_scale=w_scales[:, feats],
+                        start=(g == 0),
+                        stop=(g == PASSES - 1),
+                    )
+            acc_of[n] = acc
+
+        def out_rows(n):
+            c, part = divmod(n, GROUPS_PER_CHUNK)
+            rows = out_of[c][:].rearrange("p (r c) -> p r c", c=ROW)
+            return rows[:, part * GROUP_ROWS : (part + 1) * GROUP_ROWS]
+
+        def bias_and_products(n):
+            c, part = divmod(n, GROUPS_PER_CHUNK)
+            if part == 0:
+                out_sb = out_pool.tile([P, CHUNK_ROWS * ROW], F32)
+                out_of[c] = out_sb
+            acc = acc_of[n][:].rearrange("p (t h f) -> p t h f", t=GROUP_TILES, h=HEADS)
+            rows = out_rows(n).rearrange("p (t h) c -> p t h c", h=HEADS)
+            rotary = rope_pool.tile([P, GROUP_ROWS * 2 * PAIRS], F32)
+            by_cos = rope_pool.tile([P, GROUP_ROWS * 2 * PAIRS], F32)
+            by_sin = rope_pool.tile([P, GROUP_ROWS * 2 * PAIRS], F32)
+            halves = "p (t h e j) -> p t h e j"
+            sizes = dict(t=GROUP_TILES, h=HEADS, e=2)
+            nc.vector.tensor_tensor(
+                out=rotary[:].rearrange("p (t h f) -> p t h f", t=GROUP_TILES, h=HEADS),
+                in0=acc[:, :, :, NOPE:HEAD],
+                in1=bias_rows[:, :, :, NOPE:HEAD],
+                op=ALU.add,
+            )
+            nc.vector.tensor_tensor(
+                out=rows[:, :, :, 1 : 1 + NOPE], in0=acc[:, :, :, 0:NOPE], in1=bias_rows[:, :, :, 0:NOPE], op=ALU.add
+            )
+            nc.vector.tensor_tensor(
+                out=by_sin[:].rearrange(halves, **sizes)[:, :, :, 0],
+                in0=rotary[:].rearrange(halves, **sizes)[:, :, :, 1],
+                in1=angles(sin_neg, n, HEADS),
+                op=ALU.mult,
+            )
+            nc.vector.tensor_tensor(
+                out=by_sin[:].rearrange(halves, **sizes)[:, :, :, 1],
+                in0=rotary[:].rearrange(halves, **sizes)[:, :, :, 0],
+                in1=angles(sin_sb, n, HEADS),
+                op=ALU.mult,
+            )
+            nc.vector.tensor_tensor(
+                out=by_cos[:].rearrange("p (t q j) -> p t q j", t=GROUP_TILES, j=PAIRS),
+                in0=rotary[:].rearrange("p (t q j) -> p t q j", t=GROUP_TILES, j=PAIRS),
+                in1=angles(cos_sb, n, HEADS * 2),
+                op=ALU.mult,
+            )
+            rope_of[n] = (by_cos, by_sin)
+
+        def sum_products(n):
+            by_cos, by_sin = rope_of[n]
+            pairs = "p (r e j) -> p r j e"
+            nc.vector.tensor_tensor(
+                out=out_rows(n)[:, :, 1 + NOPE : ROW].rearrange("p r (j e) -> p r j e", e=2),
+                in0=by_cos[:].rearrange(pairs, e=2, j=PAIRS),
+                in1=by_sin[:].rearrange(pairs, e=2, j=PAIRS),
+                op=ALU.add,
+            )
+
+        def square_group(n):
+            c, part = divmod(n, GROUPS_PER_CHUNK)
+            if part == 0:
+                sums = out_pool.tile([P, CHUNK_ROWS, 1], F32)
+                squares_of[c] = sums
+            rows = out_rows(n)
+            unused = rope_pool.tile([P, GROUP_ROWS * HEAD], BF16)
+            for r in range(GROUP_ROWS):
+                nc.scalar.activation(
+                    out=unused[:, r * HEAD : (r + 1) * HEAD],
+                    in_=rows[:, r, 1:ROW],
+                    func=ACT.Square,
+                    accum_out=squares_of[c][:, part * GROUP_ROWS + r, :],
+                )
+
+        def finish_chunk(c):
+            b, part = divmod(c, CHUNKS_PER_BATCH)
+            rows = out_of[c][:].rearrange("p (r c) -> p r c", c=ROW)
+            nc.scalar.activation(out=rows[:, :, 0:1], in_=squares_of[c][:], func=ACT.Sqrt, bias=1.0)
+            dst = out[b].rearrange("(p i) h c -> p (i h c)", i=TOKENS_PER_PARTITION)
+            cols = slice(part * CHUNK_ROWS * ROW, (part + 1) * CHUNK_ROWS * ROW)
+            nc.sync.dma_start(out=dst[:, cols], in_=out_of[c][:])
+
+        def live(n):
+            return 0 <= n < N_GROUPS
+
+        for step in range(N_GROUPS + 6):
+            if live(step):
+                transpose_group(step)
+                regroup_group(step)
+            if live(step - 3):
+                bias_and_products(step - 3)
+            if live(step - 1):
+                quantise_group(step - 1)
+                multiply_group(step - 1)
+            if live(step - 3):
+                sum_products(step - 3)
+            if live(step - 5) and (step - 5) % GROUPS_PER_CHUNK == GROUPS_PER_CHUNK - 1:
+                finish_chunk((step - 5) // GROUPS_PER_CHUNK)
+            if live(step - 4):
+                square_group(step - 4)

@@ -27,6 +27,7 @@ N_CHUNKS = BATCH * CHUNKS_PER_BATCH
 N_GROUPS = N_CHUNKS * GROUPS_PER_CHUNK
 GROUP_ROWS = GROUP_TILES * HEADS
 CHUNK_ROWS = CHUNK_TILES * HEADS
+LOADS_AT_START = 16
 
 FLOPS = 2 * BATCH * SEQ * K * FEATURES
 
@@ -35,7 +36,7 @@ def tile_lorentzmla_pb_t_kernel(tc, x, freqs_cos, freqs_sin, wq_w, wq_b, out):
     nc = tc.nc
     with ExitStack() as stack:
         const = stack.enter_context(tc.tile_pool(name="const", bufs=1))
-        x_pool = stack.enter_context(tc.tile_pool(name="x", bufs=N_CHUNKS))
+        x_pool = stack.enter_context(tc.tile_pool(name="x", bufs=N_GROUPS))
         grouped_pool = stack.enter_context(tc.tile_pool(name="grouped", bufs=3))
         mx_pool = stack.enter_context(tc.tile_pool(name="mx", bufs=3))
         rope_pool = stack.enter_context(tc.tile_pool(name="rope", bufs=3))
@@ -53,24 +54,23 @@ def tile_lorentzmla_pb_t_kernel(tc, x, freqs_cos, freqs_sin, wq_w, wq_b, out):
         nc.scalar.dma_start(out=w_dst[NOPE + PAIRS : HEAD], in_=w_rotary[1])
 
         x_src = x.rearrange("b (p i) k -> b p (i k)", i=TOKENS_PER_PARTITION)
-        x_chunks = []
+        x_groups = []
 
-        def load_chunk(c):
-            b, part = divmod(c, CHUNKS_PER_BATCH)
-            x_sb = x_pool.tile([P, CHUNK_TILES * K], BF16)
-            cols = slice(part * CHUNK_TILES * K, (part + 1) * CHUNK_TILES * K)
+        def load_group(n):
+            b, part = divmod(n, TOKENS_PER_PARTITION // GROUP_TILES)
+            x_sb = x_pool.tile([P, GROUP_TILES * K], BF16)
+            cols = slice(part * GROUP_TILES * K, (part + 1) * GROUP_TILES * K)
             nc.sync.dma_start(out=x_sb[:], in_=x_src[b][:, cols])
-            x_chunks.append(x_sb)
+            x_groups.append(x_sb)
 
-        load_chunk(0)
+        for n in range(LOADS_AT_START):
+            load_group(n)
         cos_sb = const.tile([P, TOKENS_PER_PARTITION * PAIRS], BF16)
         sin_sb = const.tile([P, TOKENS_PER_PARTITION * PAIRS], BF16)
         bias_bf = const.tile([P, FEATURES], BF16)
         nc.scalar.dma_start(out=cos_sb[:], in_=freqs_cos.rearrange("(p i) j -> p (i j)", i=TOKENS_PER_PARTITION))
         nc.scalar.dma_start(out=sin_sb[:], in_=freqs_sin.rearrange("(p i) j -> p (i j)", i=TOKENS_PER_PARTITION))
         nc.scalar.dma_start(out=bias_bf[:], in_=wq_b.partition_broadcast(P))
-        for c in range(1, N_CHUNKS):
-            load_chunk(c)
 
         ident = const.tile([P, P], F32)
         make_identity(nc, ident[:])
@@ -124,11 +124,7 @@ def tile_lorentzmla_pb_t_kernel(tc, x, freqs_cos, freqs_sin, wq_w, wq_b, out):
         turned_of, grouped_of, mx_of, acc_of, rope_of, out_of, squares_of = {}, {}, {}, {}, {}, {}, {}
 
         def transpose_group(n):
-            c, part = divmod(n, GROUPS_PER_CHUNK)
-            first = part * GROUP_TILES
-            turned_of[n] = [
-                transpose_rows(x_chunks[c][:, (first + t) * K : (first + t + 1) * K]) for t in range(GROUP_TILES)
-            ]
+            turned_of[n] = [transpose_rows(x_groups[n][:, t * K : (t + 1) * K]) for t in range(GROUP_TILES)]
 
         def regroup_group(n):
             grouped = grouped_pool.tile([P, GROUP_TILES * K], BF16, align_bytes=64)
@@ -238,6 +234,8 @@ def tile_lorentzmla_pb_t_kernel(tc, x, freqs_cos, freqs_sin, wq_w, wq_b, out):
             dst = out[b].rearrange("(p i) h c -> p (i h c)", i=TOKENS_PER_PARTITION)
             cols = slice(part * CHUNK_ROWS * ROW, (part + 1) * CHUNK_ROWS * ROW)
             nc.sync.dma_start(out=dst[:, cols], in_=out_of[c][:])
+            for n in range(len(x_groups), min(len(x_groups) + GROUPS_PER_CHUNK, N_GROUPS)):
+                load_group(n)
 
         def live(n):
             return 0 <= n < N_GROUPS

@@ -48,10 +48,7 @@ def tile_lorentzmla_pb_t_kernel(tc, x, freqs_cos, freqs_sin, wq_w, wq_b, out):
         w_sb = const.tile([P, HEADS * K], BF16)
         w_dst = w_sb[:].rearrange("f (h k) -> f h k", h=HEADS)
         w_src = wq_w.rearrange("(h f) k -> f h k", h=HEADS)
-        w_rotary = w_src[NOPE:HEAD].rearrange("(j e) h k -> e j h k", e=2)
-        nc.scalar.dma_start(out=w_dst[0:NOPE], in_=w_src[0:NOPE])
-        nc.scalar.dma_start(out=w_dst[NOPE : NOPE + PAIRS], in_=w_rotary[0])
-        nc.scalar.dma_start(out=w_dst[NOPE + PAIRS : HEAD], in_=w_rotary[1])
+        nc.scalar.dma_start(out=w_dst, in_=w_src)
 
         x_src = x.rearrange("b (p i) k -> b p (i k)", i=TOKENS_PER_PARTITION)
         x_groups = []
@@ -104,22 +101,13 @@ def tile_lorentzmla_pb_t_kernel(tc, x, freqs_cos, freqs_sin, wq_w, wq_b, out):
             regroup(nc.vector.tensor_copy, w_turned, w_grouped, h)
         quantise(w_grouped, w_codes, w_scales)
 
-        sin_neg = const.tile([P, TOKENS_PER_PARTITION * PAIRS], BF16)
-        nc.vector.tensor_scalar_mul(out=sin_neg[:], in0=sin_sb[:], scalar1=-1.0)
-        bias = const.tile([P, FEATURES], F32)
-        bias_src = bias_bf[:].rearrange("p (h f) -> p h f", h=HEADS)
-        bias_dst = bias[:].rearrange("p (h f) -> p h f", h=HEADS)
-        nc.vector.tensor_copy(out=bias_dst[:, :, 0:NOPE], in_=bias_src[:, :, 0:NOPE])
-        nc.vector.tensor_copy(
-            out=bias_dst[:, :, NOPE:HEAD].rearrange("p h (e j) -> p h e j", e=2),
-            in_=bias_src[:, :, NOPE:HEAD].rearrange("p h (j e) -> p h e j", e=2),
-        )
-        bias_rows = bias[:].rearrange("p (o h f) -> p o h f", o=1, h=HEADS).to_broadcast([P, GROUP_TILES, HEADS, HEAD])
-
-        def angles(table, n, repeat):
-            i0 = (n * GROUP_TILES) % TOKENS_PER_PARTITION
-            view = table[:].rearrange("p (i o j) -> p i o j", o=1, j=PAIRS)[:, i0 : i0 + GROUP_TILES]
-            return view.to_broadcast([P, GROUP_TILES, repeat, PAIRS])
+        factors = const.tile([P, TOKENS_PER_PARTITION * PAIRS * 4], BF16)
+        factor = factors[:].rearrange("p (q e d) -> p q e d", e=2, d=2)
+        nc.vector.tensor_copy(out=factor[:, :, 0, 0], in_=cos_sb[:])
+        nc.vector.tensor_copy(out=factor[:, :, 0, 1], in_=sin_sb[:])
+        nc.vector.tensor_scalar_mul(out=factor[:, :, 1, 0], in0=sin_sb[:], scalar1=-1.0)
+        nc.vector.tensor_copy(out=factor[:, :, 1, 1], in_=cos_sb[:])
+        bias_rows = bias_bf[:].rearrange("p (o h f) -> p o h f", o=1, h=HEADS).to_broadcast([P, GROUP_TILES, HEADS, HEAD])
 
         turned_of, grouped_of, mx_of, acc_of, rope_of, out_of, squares_of = {}, {}, {}, {}, {}, {}, {}
 
@@ -161,54 +149,40 @@ def tile_lorentzmla_pb_t_kernel(tc, x, freqs_cos, freqs_sin, wq_w, wq_b, out):
             rows = out_of[c][:].rearrange("p (r c) -> p r c", c=ROW)
             return rows[:, part * GROUP_ROWS : (part + 1) * GROUP_ROWS]
 
-        def bias_and_products(n):
+        def add_bias(n):
             c, part = divmod(n, GROUPS_PER_CHUNK)
             if part == 0:
                 out_sb = out_pool.tile([P, CHUNK_ROWS * ROW], F32)
                 out_of[c] = out_sb
-            acc = acc_of[n][:].rearrange("p (t h f) -> p t h f", t=GROUP_TILES, h=HEADS)
-            rows = out_rows(n).rearrange("p (t h) c -> p t h c", h=HEADS)
-            rotary = rope_pool.tile([P, GROUP_ROWS * 2 * PAIRS], F32)
-            by_cos = rope_pool.tile([P, GROUP_ROWS * 2 * PAIRS], F32)
-            by_sin = rope_pool.tile([P, GROUP_ROWS * 2 * PAIRS], F32)
-            halves = "p (t h e j) -> p t h e j"
-            sizes = dict(t=GROUP_TILES, h=HEADS, e=2)
             nc.vector.tensor_tensor(
-                out=rotary[:].rearrange("p (t h f) -> p t h f", t=GROUP_TILES, h=HEADS),
-                in0=acc[:, :, :, NOPE:HEAD],
-                in1=bias_rows[:, :, :, NOPE:HEAD],
+                out=out_rows(n).rearrange("p (t h) c -> p t h c", h=HEADS)[:, :, :, 1:ROW],
+                in0=acc_of[n][:].rearrange("p (t h f) -> p t h f", t=GROUP_TILES, h=HEADS),
+                in1=bias_rows,
                 op=ALU.add,
             )
+
+        def rotary(n):
+            return out_rows(n).rearrange("p (t h) c -> p t h c", h=HEADS)[:, :, :, 1 + NOPE : ROW]
+
+        def multiply_factors(n):
+            products = rope_pool.tile([P, GROUP_ROWS * PAIRS * 4], F32)
+            shape = [P, GROUP_TILES, HEADS, 2 * PAIRS, 2]
+            i0 = (n * GROUP_TILES) % TOKENS_PER_PARTITION
+            table = factors[:].rearrange("p (i o a d) -> p i o a d", o=1, a=2 * PAIRS, d=2)
             nc.vector.tensor_tensor(
-                out=rows[:, :, :, 1 : 1 + NOPE], in0=acc[:, :, :, 0:NOPE], in1=bias_rows[:, :, :, 0:NOPE], op=ALU.add
-            )
-            nc.vector.tensor_tensor(
-                out=by_sin[:].rearrange(halves, **sizes)[:, :, :, 0],
-                in0=rotary[:].rearrange(halves, **sizes)[:, :, :, 1],
-                in1=angles(sin_neg, n, HEADS),
+                out=products[:].rearrange("p (t h a d) -> p t h a d", t=GROUP_TILES, h=HEADS, d=2),
+                in0=rotary(n).rearrange("p t h (a o) -> p t h a o", o=1).to_broadcast(shape),
+                in1=table[:, i0 : i0 + GROUP_TILES].to_broadcast(shape),
                 op=ALU.mult,
             )
-            nc.vector.tensor_tensor(
-                out=by_sin[:].rearrange(halves, **sizes)[:, :, :, 1],
-                in0=rotary[:].rearrange(halves, **sizes)[:, :, :, 0],
-                in1=angles(sin_sb, n, HEADS),
-                op=ALU.mult,
-            )
-            nc.vector.tensor_tensor(
-                out=by_cos[:].rearrange("p (t q j) -> p t q j", t=GROUP_TILES, j=PAIRS),
-                in0=rotary[:].rearrange("p (t q j) -> p t q j", t=GROUP_TILES, j=PAIRS),
-                in1=angles(cos_sb, n, HEADS * 2),
-                op=ALU.mult,
-            )
-            rope_of[n] = (by_cos, by_sin)
+            rope_of[n] = products
 
         def sum_products(n):
-            by_cos, by_sin = rope_of[n]
-            pairs = "p (r e j) -> p r j e"
+            halves = rope_of[n][:].rearrange("p (t h j e d) -> p t h j e d", t=GROUP_TILES, h=HEADS, e=2, d=2)
             nc.vector.tensor_tensor(
-                out=out_rows(n)[:, :, 1 + NOPE : ROW].rearrange("p r (j e) -> p r j e", e=2),
-                in0=by_cos[:].rearrange(pairs, e=2, j=PAIRS),
-                in1=by_sin[:].rearrange(pairs, e=2, j=PAIRS),
+                out=rotary(n).rearrange("p t h (j d) -> p t h j d", d=2),
+                in0=halves[:, :, :, :, 0],
+                in1=halves[:, :, :, :, 1],
                 op=ALU.add,
             )
 
@@ -240,18 +214,20 @@ def tile_lorentzmla_pb_t_kernel(tc, x, freqs_cos, freqs_sin, wq_w, wq_b, out):
         def live(n):
             return 0 <= n < N_GROUPS
 
-        for step in range(N_GROUPS + 6):
+        for step in range(N_GROUPS + 7):
             if live(step):
                 transpose_group(step)
                 regroup_group(step)
             if live(step - 3):
-                bias_and_products(step - 3)
+                add_bias(step - 3)
+            if live(step - 4):
+                sum_products(step - 4)
             if live(step - 1):
                 quantise_group(step - 1)
                 multiply_group(step - 1)
             if live(step - 3):
-                sum_products(step - 3)
-            if live(step - 5) and (step - 5) % GROUPS_PER_CHUNK == GROUPS_PER_CHUNK - 1:
-                finish_chunk((step - 5) // GROUPS_PER_CHUNK)
-            if live(step - 4):
-                square_group(step - 4)
+                multiply_factors(step - 3)
+            if live(step - 6) and (step - 6) % GROUPS_PER_CHUNK == GROUPS_PER_CHUNK - 1:
+                finish_chunk((step - 6) // GROUPS_PER_CHUNK)
+            if live(step - 5):
+                square_group(step - 5)

@@ -37,18 +37,13 @@ def tile_lorentzmla_pb_t_kernel(tc, x, freqs_cos, freqs_sin, wq_w, wq_b, out):
     with ExitStack() as stack:
         const = stack.enter_context(tc.tile_pool(name="const", bufs=1))
         x_pool = stack.enter_context(tc.tile_pool(name="x", bufs=N_GROUPS))
-        grouped_pool = stack.enter_context(tc.tile_pool(name="grouped", bufs=3))
-        mx_pool = stack.enter_context(tc.tile_pool(name="mx", bufs=3))
+        grouped_pool = stack.enter_context(tc.tile_pool(name="grouped", bufs=6))
+        mx_pool = stack.enter_context(tc.tile_pool(name="mx", bufs=6))
         rope_pool = stack.enter_context(tc.tile_pool(name="rope", bufs=3))
         out_pool = stack.enter_context(tc.tile_pool(name="out", bufs=6))
         turned_pool = stack.enter_context(tc.psum_pool(name="turned", bufs=4))
         acc_pool = stack.enter_context(tc.psum_pool(name="acc", bufs=4))
         stack.enter_context(tc.manual_schedule())
-
-        w_sb = const.tile([P, HEADS * K], BF16)
-        w_dst = w_sb[:].rearrange("f (h k) -> f h k", h=HEADS)
-        w_src = wq_w.rearrange("(h f) k -> f h k", h=HEADS)
-        nc.scalar.dma_start(out=w_dst, in_=w_src)
 
         x_src = x.rearrange("b (p i) k -> b p (i k)", i=TOKENS_PER_PARTITION)
         x_groups = []
@@ -60,11 +55,15 @@ def tile_lorentzmla_pb_t_kernel(tc, x, freqs_cos, freqs_sin, wq_w, wq_b, out):
             nc.sync.dma_start(out=x_sb[:], in_=x_src[b][:, cols])
             x_groups.append(x_sb)
 
-        for n in range(LOADS_AT_START):
-            load_group(n)
+        w_sb = const.tile([P, HEADS * K], BF16)
         cos_sb = const.tile([P, TOKENS_PER_PARTITION * PAIRS], BF16)
         sin_sb = const.tile([P, TOKENS_PER_PARTITION * PAIRS], BF16)
         bias_bf = const.tile([P, FEATURES], BF16)
+        nc.scalar.dma_start(
+            out=w_sb[:].rearrange("f (h k) -> f h k", h=HEADS), in_=wq_w.rearrange("(h f) k -> f h k", h=HEADS)
+        )
+        for n in range(LOADS_AT_START):
+            load_group(n)
         nc.scalar.dma_start(out=cos_sb[:], in_=freqs_cos.rearrange("(p i) j -> p (i j)", i=TOKENS_PER_PARTITION))
         nc.scalar.dma_start(out=sin_sb[:], in_=freqs_sin.rearrange("(p i) j -> p (i j)", i=TOKENS_PER_PARTITION))
         nc.scalar.dma_start(out=bias_bf[:], in_=wq_b.partition_broadcast(P))
@@ -111,6 +110,9 @@ def tile_lorentzmla_pb_t_kernel(tc, x, freqs_cos, freqs_sin, wq_w, wq_b, out):
 
         turned_of, grouped_of, mx_of, acc_of, rope_of, out_of, squares_of = {}, {}, {}, {}, {}, {}, {}
 
+        def groups(c):
+            return range(c * GROUPS_PER_CHUNK, (c + 1) * GROUPS_PER_CHUNK)
+
         def transpose_group(n):
             turned_of[n] = [transpose_rows(x_groups[n][:, t * K : (t + 1) * K]) for t in range(GROUP_TILES)]
 
@@ -144,10 +146,8 @@ def tile_lorentzmla_pb_t_kernel(tc, x, freqs_cos, freqs_sin, wq_w, wq_b, out):
                     )
             acc_of[n] = acc
 
-        def out_rows(n):
-            c, part = divmod(n, GROUPS_PER_CHUNK)
-            rows = out_of[c][:].rearrange("p (r c) -> p r c", c=ROW)
-            return rows[:, part * GROUP_ROWS : (part + 1) * GROUP_ROWS]
+        def rows_of(c):
+            return out_of[c][:].rearrange("p (t h c) -> p t h c", h=HEADS, c=ROW)
 
         def add_bias(n):
             c, part = divmod(n, GROUPS_PER_CHUNK)
@@ -155,50 +155,45 @@ def tile_lorentzmla_pb_t_kernel(tc, x, freqs_cos, freqs_sin, wq_w, wq_b, out):
                 out_sb = out_pool.tile([P, CHUNK_ROWS * ROW], F32)
                 out_of[c] = out_sb
             nc.vector.tensor_tensor(
-                out=out_rows(n).rearrange("p (t h) c -> p t h c", h=HEADS)[:, :, :, 1:ROW],
+                out=rows_of(c)[:, part * GROUP_TILES : (part + 1) * GROUP_TILES, :, 1:ROW],
                 in0=acc_of[n][:].rearrange("p (t h f) -> p t h f", t=GROUP_TILES, h=HEADS),
                 in1=bias_rows,
                 op=ALU.add,
             )
 
-        def rotary(n):
-            return out_rows(n).rearrange("p (t h) c -> p t h c", h=HEADS)[:, :, :, 1 + NOPE : ROW]
-
-        def multiply_factors(n):
-            products = rope_pool.tile([P, GROUP_ROWS * PAIRS * 4], F32)
-            shape = [P, GROUP_TILES, HEADS, 2 * PAIRS, 2]
-            i0 = (n * GROUP_TILES) % TOKENS_PER_PARTITION
+        def multiply_factors(c):
+            products = rope_pool.tile([P, CHUNK_ROWS * PAIRS * 4], F32)
+            shape = [P, CHUNK_TILES, HEADS, 2 * PAIRS, 2]
+            i0 = (c * CHUNK_TILES) % TOKENS_PER_PARTITION
             table = factors[:].rearrange("p (i o a d) -> p i o a d", o=1, a=2 * PAIRS, d=2)
             nc.vector.tensor_tensor(
-                out=products[:].rearrange("p (t h a d) -> p t h a d", t=GROUP_TILES, h=HEADS, d=2),
-                in0=rotary(n).rearrange("p t h (a o) -> p t h a o", o=1).to_broadcast(shape),
-                in1=table[:, i0 : i0 + GROUP_TILES].to_broadcast(shape),
+                out=products[:].rearrange("p (t h a d) -> p t h a d", t=CHUNK_TILES, h=HEADS, d=2),
+                in0=rows_of(c)[:, :, :, 1 + NOPE : ROW].rearrange("p t h (a o) -> p t h a o", o=1).to_broadcast(shape),
+                in1=table[:, i0 : i0 + CHUNK_TILES].to_broadcast(shape),
                 op=ALU.mult,
             )
-            rope_of[n] = products
+            rope_of[c] = products
 
-        def sum_products(n):
-            halves = rope_of[n][:].rearrange("p (t h j e d) -> p t h j e d", t=GROUP_TILES, h=HEADS, e=2, d=2)
+        def sum_products(c):
+            halves = rope_of[c][:].rearrange("p (t h j e d) -> p t h j e d", t=CHUNK_TILES, h=HEADS, e=2, d=2)
             nc.vector.tensor_tensor(
-                out=rotary(n).rearrange("p t h (j d) -> p t h j d", d=2),
+                out=rows_of(c)[:, :, :, 1 + NOPE : ROW].rearrange("p t h (j d) -> p t h j d", d=2),
                 in0=halves[:, :, :, :, 0],
                 in1=halves[:, :, :, :, 1],
                 op=ALU.add,
             )
 
-        def square_group(n):
-            c, part = divmod(n, GROUPS_PER_CHUNK)
-            if part == 0:
-                sums = out_pool.tile([P, CHUNK_ROWS, 1], F32)
-                squares_of[c] = sums
-            rows = out_rows(n)
-            unused = rope_pool.tile([P, GROUP_ROWS * HEAD], BF16)
-            for r in range(GROUP_ROWS):
+        def square_chunk(c):
+            sums = out_pool.tile([P, CHUNK_ROWS, 1], F32)
+            squares_of[c] = sums
+            rows = out_of[c][:].rearrange("p (r c) -> p r c", c=ROW)
+            unused = rope_pool.tile([P, CHUNK_ROWS * HEAD], BF16)
+            for r in range(CHUNK_ROWS):
                 nc.scalar.activation(
                     out=unused[:, r * HEAD : (r + 1) * HEAD],
                     in_=rows[:, r, 1:ROW],
                     func=ACT.Square,
-                    accum_out=squares_of[c][:, part * GROUP_ROWS + r, :],
+                    accum_out=sums[:, r, :],
                 )
 
         def finish_chunk(c):
@@ -211,23 +206,29 @@ def tile_lorentzmla_pb_t_kernel(tc, x, freqs_cos, freqs_sin, wq_w, wq_b, out):
             for n in range(len(x_groups), min(len(x_groups) + GROUPS_PER_CHUNK, N_GROUPS)):
                 load_group(n)
 
-        def live(n):
-            return 0 <= n < N_GROUPS
+        def live(c):
+            return 0 <= c < N_CHUNKS
 
-        for step in range(N_GROUPS + 7):
+        for step in range(N_CHUNKS + 7):
+            if live(step - 6):
+                finish_chunk(step - 6)
             if live(step):
-                transpose_group(step)
-                regroup_group(step)
+                for n in groups(step):
+                    transpose_group(n)
+                    regroup_group(n)
+            if live(step - 2):
+                for n in groups(step - 2):
+                    multiply_group(n)
             if live(step - 3):
-                add_bias(step - 3)
+                add_bias(groups(step - 3)[0])
             if live(step - 4):
                 sum_products(step - 4)
+            if live(step - 3):
+                add_bias(groups(step - 3)[1])
             if live(step - 1):
-                quantise_group(step - 1)
-                multiply_group(step - 1)
+                for n in groups(step - 1):
+                    quantise_group(n)
             if live(step - 3):
                 multiply_factors(step - 3)
-            if live(step - 6) and (step - 6) % GROUPS_PER_CHUNK == GROUPS_PER_CHUNK - 1:
-                finish_chunk((step - 6) // GROUPS_PER_CHUNK)
             if live(step - 5):
-                square_group(step - 5)
+                square_chunk(step - 5)

@@ -28,6 +28,7 @@ N_GROUPS = N_CHUNKS * GROUPS_PER_CHUNK
 GROUP_ROWS = GROUP_TILES * HEADS
 CHUNK_ROWS = CHUNK_TILES * HEADS
 LOADS_AT_START = 16
+SPINS_AT_START = 6
 
 FLOPS = 2 * BATCH * SEQ * K * FEATURES
 
@@ -75,6 +76,16 @@ def tile_lorentzmla_pb_t_kernel(tc, x, freqs_cos, freqs_sin, wq_w, wq_b, out):
         nc.vector.memset(warm[:], 1.0)
         nc.scalar.sqrt(out=warm[:], in_=warm[:])
 
+        ones = const.tile([P, GROUP_TILES * FEATURES], BF16)
+        nc.vector.memset(ones[:], 1.0)
+
+        def spin_tensor(times):
+            acc = acc_pool.tile([P, GROUP_TILES * FEATURES], F32)
+            for i in range(times):
+                nc.tensor.matmul(out=acc[:], lhsT=ones[:, 0:P], rhs=ones[:], start=True, stop=True)
+
+        spin_tensor(SPINS_AT_START)
+
         def transpose_rows(rows_bf16):
             words = rows_bf16.bitcast(F32)
             turned = turned_pool.tile([P, WORDS], F32)
@@ -98,6 +109,7 @@ def tile_lorentzmla_pb_t_kernel(tc, x, freqs_cos, freqs_sin, wq_w, wq_b, out):
         for h in range(HEADS):
             w_turned = transpose_rows(w_sb[:, h * K : (h + 1) * K])
             regroup(nc.vector.tensor_copy, w_turned, w_grouped, h)
+        spin_tensor(1)
         quantise(w_grouped, w_codes, w_scales)
 
         factors = const.tile([P, TOKENS_PER_PARTITION * PAIRS * 4], BF16)
@@ -215,6 +227,8 @@ def tile_lorentzmla_pb_t_kernel(tc, x, freqs_cos, freqs_sin, wq_w, wq_b, out):
             if live(step):
                 for n in groups(step):
                     transpose_group(n)
+                    if step < 2:
+                        spin_tensor(1)
                     regroup_group(n)
             if live(step - 2):
                 for n in groups(step - 2):

@@ -224,15 +224,14 @@ def tile_lorentzmla_pb_t_kernel(tc, x, freqs_cos, freqs_sin, wq_w, wq_b, out):
         for step in range(N_CHUNKS + 7):
             if live(step - 6):
                 finish_chunk(step - 6)
-            if live(step):
-                for n in groups(step):
-                    transpose_group(n)
-                    if step < 2:
-                        spin_tensor(1)
-                    regroup_group(n)
-            if live(step - 2):
-                for n in groups(step - 2):
-                    multiply_group(n)
+            for part in range(GROUPS_PER_CHUNK):
+                if live(step):
+                    transpose_group(groups(step)[part])
+                    regroup_group(groups(step)[part])
+                if live(step - 2):
+                    multiply_group(groups(step - 2)[part])
+                elif step < 2:
+                    spin_tensor(1)
             if live(step - 3):
                 add_bias(groups(step - 3)[0])
             if live(step - 4):

@@ -188,7 +188,7 @@ def tile_lorentzmla_pb_t_kernel(tc, x, freqs_cos, freqs_sin, wq_w, wq_b, out):
 
         def sum_products(c):
             halves = rope_of[c][:].rearrange("p (t h j e d) -> p t h j e d", t=CHUNK_TILES, h=HEADS, e=2, d=2)
-            nc.vector.tensor_tensor(
+            nc.gpsimd.tensor_tensor(
                 out=rows_of(c)[:, :, :, 1 + NOPE : ROW].rearrange("p t h (j d) -> p t h j d", d=2),
                 in0=halves[:, :, :, :, 0],
                 in1=halves[:, :, :, :, 1],
@@ -221,9 +221,9 @@ def tile_lorentzmla_pb_t_kernel(tc, x, freqs_cos, freqs_sin, wq_w, wq_b, out):
         def live(c):
             return 0 <= c < N_CHUNKS
 
-        for step in range(N_CHUNKS + 7):
-            if live(step - 6):
-                finish_chunk(step - 6)
+        for step in range(N_CHUNKS + 6):
+            if live(step - 5):
+                finish_chunk(step - 5)
             for part in range(GROUPS_PER_CHUNK):
                 if live(step):
                     transpose_group(groups(step)[part])
@@ -233,15 +233,13 @@ def tile_lorentzmla_pb_t_kernel(tc, x, freqs_cos, freqs_sin, wq_w, wq_b, out):
                 elif step < 2:
                     spin_tensor(1)
             if live(step - 3):
-                add_bias(groups(step - 3)[0])
-            if live(step - 4):
-                sum_products(step - 4)
-            if live(step - 3):
-                add_bias(groups(step - 3)[1])
+                for n in groups(step - 3):
+                    add_bias(n)
             if live(step - 1):
                 for n in groups(step - 1):
                     quantise_group(n)
             if live(step - 3):
                 multiply_factors(step - 3)
-            if live(step - 5):
-                square_chunk(step - 5)
+                sum_products(step - 3)
+            if live(step - 4):
+                square_chunk(step - 4)

@@ -29,6 +29,8 @@ GROUP_ROWS = GROUP_TILES * HEADS
 CHUNK_ROWS = CHUNK_TILES * HEADS
 LOADS_AT_START = 16
 SPINS_AT_START = 6
+LEAD = 3
+W_AFTER = 1
 
 FLOPS = 2 * BATCH * SEQ * K * FEATURES
 
@@ -46,6 +48,14 @@ def tile_lorentzmla_pb_t_kernel(tc, x, freqs_cos, freqs_sin, wq_w, wq_b, out):
         acc_pool = stack.enter_context(tc.psum_pool(name="acc", bufs=4))
         stack.enter_context(tc.manual_schedule())
 
+        cos_sb = const.tile([P, TOKENS_PER_PARTITION * PAIRS], BF16)
+        sin_sb = const.tile([P, TOKENS_PER_PARTITION * PAIRS], BF16)
+        nc.scalar.dma_start(out=cos_sb[:], in_=freqs_cos.rearrange("(p i) j -> p (i j)", i=TOKENS_PER_PARTITION))
+        nc.scalar.dma_start(out=sin_sb[:], in_=freqs_sin.rearrange("(p i) j -> p (i j)", i=TOKENS_PER_PARTITION))
+        bias_row = const.tile([P, FEATURES], BF16)
+        nc.vector.memset(bias_row[:], 1.0)
+        nc.scalar.dma_start(out=bias_row[0:1, :], in_=wq_b.rearrange("(o f) -> o f", o=1))
+
         x_src = x.rearrange("b (p i) k -> b p (i k)", i=TOKENS_PER_PARTITION)
         x_groups = []
 
@@ -57,17 +67,12 @@ def tile_lorentzmla_pb_t_kernel(tc, x, freqs_cos, freqs_sin, wq_w, wq_b, out):
             x_groups.append(x_sb)
 
         w_sb = const.tile([P, HEADS * K], BF16)
-        cos_sb = const.tile([P, TOKENS_PER_PARTITION * PAIRS], BF16)
-        sin_sb = const.tile([P, TOKENS_PER_PARTITION * PAIRS], BF16)
-        bias_bf = const.tile([P, FEATURES], BF16)
-        nc.scalar.dma_start(
-            out=w_sb[:].rearrange("f (h k) -> f h k", h=HEADS), in_=wq_w.rearrange("(h f) k -> f h k", h=HEADS)
-        )
         for n in range(LOADS_AT_START):
             load_group(n)
-        nc.scalar.dma_start(out=cos_sb[:], in_=freqs_cos.rearrange("(p i) j -> p (i j)", i=TOKENS_PER_PARTITION))
-        nc.scalar.dma_start(out=sin_sb[:], in_=freqs_sin.rearrange("(p i) j -> p (i j)", i=TOKENS_PER_PARTITION))
-        nc.scalar.dma_start(out=bias_bf[:], in_=wq_b.partition_broadcast(P))
+            if n == W_AFTER:
+                nc.sync.dma_start(
+                    out=w_sb[:].rearrange("f (h k) -> f h k", h=HEADS), in_=wq_w.rearrange("(h f) k -> f h k", h=HEADS)
+                )
 
         ident = const.tile([P, P], F32)
         make_identity(nc, ident[:])
@@ -103,22 +108,31 @@ def tile_lorentzmla_pb_t_kernel(tc, x, freqs_cos, freqs_sin, wq_w, wq_b, out):
         def quantise(grouped, codes, scales):
             nc.vector.quantize_mx(out=codes[:].bitcast(FP8X4), scales=scales[:], in_=grouped[:])
 
-        w_grouped = const.tile([P, GROUP_TILES * K], BF16, align_bytes=64)
-        w_codes = const.tile([P, PASSES * FEATURES], U32, align_bytes=64)
-        w_scales = const.tile([P, PASSES * FEATURES], U8, align_bytes=64)
-        for h in range(HEADS):
-            w_turned = transpose_rows(w_sb[:, h * K : (h + 1) * K])
-            regroup(nc.vector.tensor_copy, w_turned, w_grouped, h)
-        spin_tensor(1)
-        quantise(w_grouped, w_codes, w_scales)
-
         factors = const.tile([P, TOKENS_PER_PARTITION * PAIRS * 4], BF16)
         factor = factors[:].rearrange("p (q e d) -> p q e d", e=2, d=2)
         nc.vector.tensor_copy(out=factor[:, :, 0, 0], in_=cos_sb[:])
         nc.vector.tensor_copy(out=factor[:, :, 0, 1], in_=sin_sb[:])
         nc.vector.tensor_scalar_mul(out=factor[:, :, 1, 0], in0=sin_sb[:], scalar1=-1.0)
         nc.vector.tensor_copy(out=factor[:, :, 1, 1], in_=cos_sb[:])
-        bias_rows = bias_bf[:].rearrange("p (o h f) -> p o h f", o=1, h=HEADS).to_broadcast([P, GROUP_TILES, HEADS, HEAD])
+        first = const.tile([P, 1], BF16)
+        nc.vector.tensor_copy(out=first[:], in_=ident[:, 0:1])
+        bias = const.tile([P, FEATURES], F32)
+        bias_rows = bias[:].rearrange("p (o h f) -> p o h f", o=1, h=HEADS).to_broadcast([P, GROUP_TILES, HEADS, HEAD])
+
+        w_grouped = const.tile([P, GROUP_TILES * K], BF16, align_bytes=64)
+        w_codes = const.tile([P, PASSES * FEATURES], U32, align_bytes=64)
+        w_scales = const.tile([P, PASSES * FEATURES], U8, align_bytes=64)
+
+        def prepare_weights():
+            for h in range(HEADS):
+                w_turned = transpose_rows(w_sb[:, h * K : (h + 1) * K])
+                regroup(nc.vector.tensor_copy, w_turned, w_grouped, h)
+            quantise(w_grouped, w_codes, w_scales)
+            acc = acc_pool.tile([P, GROUP_TILES * FEATURES], F32)
+            nc.tensor.matmul(
+                out=acc[:, 0:FEATURES], lhsT=first[:].to_broadcast([P, P]), rhs=bias_row[:], start=True, stop=True
+            )
+            nc.scalar.copy(out=bias[:], in_=acc[:, 0:FEATURES])
 
         turned_of, grouped_of, mx_of, acc_of, rope_of, out_of, squares_of = {}, {}, {}, {}, {}, {}, {}
 
@@ -188,24 +202,27 @@ def tile_lorentzmla_pb_t_kernel(tc, x, freqs_cos, freqs_sin, wq_w, wq_b, out):
 
         def sum_products(c):
             halves = rope_of[c][:].rearrange("p (t h j e d) -> p t h j e d", t=CHUNK_TILES, h=HEADS, e=2, d=2)
-            nc.gpsimd.tensor_tensor(
+            engine = nc.vector if c == N_CHUNKS - 1 else nc.gpsimd
+            engine.tensor_tensor(
                 out=rows_of(c)[:, :, :, 1 + NOPE : ROW].rearrange("p t h (j d) -> p t h j d", d=2),
                 in0=halves[:, :, :, :, 0],
                 in1=halves[:, :, :, :, 1],
                 op=ALU.add,
             )
 
-        def square_chunk(c):
-            sums = out_pool.tile([P, CHUNK_ROWS, 1], F32)
-            squares_of[c] = sums
+        def square_group(n):
+            c, part = divmod(n, GROUPS_PER_CHUNK)
+            if part == 0:
+                sums = out_pool.tile([P, CHUNK_ROWS, 1], F32)
+                squares_of[c] = sums
             rows = out_of[c][:].rearrange("p (r c) -> p r c", c=ROW)
-            unused = rope_pool.tile([P, CHUNK_ROWS * HEAD], BF16)
-            for r in range(CHUNK_ROWS):
+            unused = rope_pool.tile([P, GROUP_ROWS * HEAD], BF16)
+            for r in range(GROUP_ROWS):
                 nc.scalar.activation(
                     out=unused[:, r * HEAD : (r + 1) * HEAD],
-                    in_=rows[:, r, 1:ROW],
+                    in_=rows[:, part * GROUP_ROWS + r, 1:ROW],
                     func=ACT.Square,
-                    accum_out=sums[:, r, :],
+                    accum_out=squares_of[c][:, part * GROUP_ROWS + r, :],
                 )
 
         def finish_chunk(c):
@@ -218,28 +235,31 @@ def tile_lorentzmla_pb_t_kernel(tc, x, freqs_cos, freqs_sin, wq_w, wq_b, out):
             for n in range(len(x_groups), min(len(x_groups) + GROUPS_PER_CHUNK, N_GROUPS)):
                 load_group(n)
 
-        def live(c):
-            return 0 <= c < N_CHUNKS
+        def live(n):
+            return 0 <= n < N_GROUPS
 
-        for step in range(N_CHUNKS + 6):
-            if live(step - 5):
-                finish_chunk(step - 5)
-            for part in range(GROUPS_PER_CHUNK):
-                if live(step):
-                    transpose_group(groups(step)[part])
-                    regroup_group(groups(step)[part])
-                if live(step - 2):
-                    multiply_group(groups(step - 2)[part])
-                elif step < 2:
-                    spin_tensor(1)
-            if live(step - 3):
-                for n in groups(step - 3):
-                    add_bias(n)
-            if live(step - 1):
-                for n in groups(step - 1):
-                    quantise_group(n)
-            if live(step - 3):
-                multiply_factors(step - 3)
-                sum_products(step - 3)
-            if live(step - 4):
-                square_chunk(step - 4)
+        for n in range(N_GROUPS + LEAD + 5):
+            if live(n):
+                transpose_group(n)
+                regroup_group(n)
+            if n == W_AFTER:
+                prepare_weights()
+            if live(n - LEAD):
+                multiply_group(n - LEAD)
+            elif n < LEAD:
+                spin_tensor(1)
+            c, part = divmod(n - LEAD - 1, GROUPS_PER_CHUNK)
+            if part == 0:
+                if 0 <= c < N_CHUNKS:
+                    for g in groups(c):
+                        add_bias(g)
+                for g in (n - 1, n):
+                    if live(g):
+                        quantise_group(g)
+                if 0 <= c < N_CHUNKS:
+                    multiply_factors(c)
+                    sum_products(c)
+            if live(n - LEAD - 3):
+                square_group(n - LEAD - 3)
+                if (n - LEAD - 3) % GROUPS_PER_CHUNK == GROUPS_PER_CHUNK - 1:
+                    finish_chunk((n - LEAD - 3) // GROUPS_PER_CHUNK)

@@ -39,7 +39,7 @@ def tile_lorentzmla_pb_t_kernel(tc, x, freqs_cos, freqs_sin, wq_w, wq_b, out):
     nc = tc.nc
     with ExitStack() as stack:
         const = stack.enter_context(tc.tile_pool(name="const", bufs=1))
-        x_pool = stack.enter_context(tc.tile_pool(name="x", bufs=N_GROUPS))
+        x_pool = stack.enter_context(tc.tile_pool(name="x", bufs=N_GROUPS - 1))
         grouped_pool = stack.enter_context(tc.tile_pool(name="grouped", bufs=6))
         mx_pool = stack.enter_context(tc.tile_pool(name="mx", bufs=6))
         rope_pool = stack.enter_context(tc.tile_pool(name="rope", bufs=3))
@@ -57,17 +57,23 @@ def tile_lorentzmla_pb_t_kernel(tc, x, freqs_cos, freqs_sin, wq_w, wq_b, out):
         nc.scalar.dma_start(out=bias_row[0:1, :], in_=wq_b.rearrange("(o f) -> o f", o=1))
 
         x_src = x.rearrange("b (p i) k -> b p (i k)", i=TOKENS_PER_PARTITION)
-        x_groups = []
+        x_tiles = {}
 
         def load_group(n):
             b, part = divmod(n, TOKENS_PER_PARTITION // GROUP_TILES)
             x_sb = x_pool.tile([P, GROUP_TILES * K], BF16)
             cols = slice(part * GROUP_TILES * K, (part + 1) * GROUP_TILES * K)
             nc.sync.dma_start(out=x_sb[:], in_=x_src[b][:, cols])
-            x_groups.append(x_sb)
+            for t in range(GROUP_TILES):
+                x_tiles[(n, t)] = x_sb[:, t * K : (t + 1) * K]
+
+        for t in range(GROUP_TILES):
+            x_first = const.tile([P, K], BF16, name="x_first_%d" % t)
+            nc.sync.dma_start(out=x_first[:], in_=x_src[0][:, t * K : (t + 1) * K])
+            x_tiles[(0, t)] = x_first[:]
 
         w_sb = const.tile([P, HEADS * K], BF16)
-        for n in range(LOADS_AT_START):
+        for n in range(1, LOADS_AT_START):
             load_group(n)
             if n == W_AFTER:
                 nc.sync.dma_start(
@@ -140,7 +146,7 @@ def tile_lorentzmla_pb_t_kernel(tc, x, freqs_cos, freqs_sin, wq_w, wq_b, out):
             return range(c * GROUPS_PER_CHUNK, (c + 1) * GROUPS_PER_CHUNK)
 
         def transpose_group(n):
-            turned_of[n] = [transpose_rows(x_groups[n][:, t * K : (t + 1) * K]) for t in range(GROUP_TILES)]
+            turned_of[n] = [transpose_rows(x_tiles[(n, t)]) for t in range(GROUP_TILES)]
 
         def regroup_group(n):
             grouped = grouped_pool.tile([P, GROUP_TILES * K], BF16, align_bytes=64)
@@ -218,12 +224,15 @@ def tile_lorentzmla_pb_t_kernel(tc, x, freqs_cos, freqs_sin, wq_w, wq_b, out):
             rows = out_of[c][:].rearrange("p (r c) -> p r c", c=ROW)
             unused = rope_pool.tile([P, GROUP_ROWS * HEAD], BF16)
             for r in range(GROUP_ROWS):
-                nc.scalar.activation(
-                    out=unused[:, r * HEAD : (r + 1) * HEAD],
-                    in_=rows[:, part * GROUP_ROWS + r, 1:ROW],
-                    func=ACT.Square,
-                    accum_out=squares_of[c][:, part * GROUP_ROWS + r, :],
-                )
+                row = rows[:, part * GROUP_ROWS + r, 1:ROW]
+                squares = unused[:, r * HEAD : (r + 1) * HEAD]
+                total = squares_of[c][:, part * GROUP_ROWS + r, :]
+                if n == N_GROUPS - 1:
+                    nc.vector.scalar_tensor_tensor(
+                        out=squares, in0=row, scalar=1.0, in1=row, op0=ALU.mult, op1=ALU.mult, accum_out=total
+                    )
+                else:
+                    nc.scalar.activation(out=squares, in_=row, func=ACT.Square, accum_out=total)
 
         def finish_chunk(c):
             b, part = divmod(c, CHUNKS_PER_BATCH)
@@ -232,7 +241,8 @@ def tile_lorentzmla_pb_t_kernel(tc, x, freqs_cos, freqs_sin, wq_w, wq_b, out):
             dst = out[b].rearrange("(p i) h c -> p (i h c)", i=TOKENS_PER_PARTITION)
             cols = slice(part * CHUNK_ROWS * ROW, (part + 1) * CHUNK_ROWS * ROW)
             nc.sync.dma_start(out=dst[:, cols], in_=out_of[c][:])
-            for n in range(len(x_groups), min(len(x_groups) + GROUPS_PER_CHUNK, N_GROUPS)):
+            loaded = len(x_tiles) // GROUP_TILES
+            for n in range(loaded, min(loaded + GROUPS_PER_CHUNK, N_GROUPS)):
                 load_group(n)
 
         def live(n):

@@ -28,7 +28,7 @@ N_GROUPS = N_CHUNKS * GROUPS_PER_CHUNK
 GROUP_ROWS = GROUP_TILES * HEADS
 CHUNK_ROWS = CHUNK_TILES * HEADS
 LOADS_AT_START = 16
-SPINS_AT_START = 6
+SPINS_AT_START = 3
 LEAD = 3
 W_AFTER = 1
 
@@ -47,6 +47,9 @@ def tile_lorentzmla_pb_t_kernel(tc, x, freqs_cos, freqs_sin, wq_w, wq_b, out):
         turned_pool = stack.enter_context(tc.psum_pool(name="turned", bufs=4))
         acc_pool = stack.enter_context(tc.psum_pool(name="acc", bufs=4))
         stack.enter_context(tc.manual_schedule())
+
+        ones = const.tile([P, GROUP_TILES * FEATURES], BF16)
+        nc.vector.memset(ones[:], 1.0)
 
         cos_sb = const.tile([P, TOKENS_PER_PARTITION * PAIRS], BF16)
         sin_sb = const.tile([P, TOKENS_PER_PARTITION * PAIRS], BF16)
@@ -86,9 +89,6 @@ def tile_lorentzmla_pb_t_kernel(tc, x, freqs_cos, freqs_sin, wq_w, wq_b, out):
         warm = const.tile([P, 1], F32)
         nc.vector.memset(warm[:], 1.0)
         nc.scalar.sqrt(out=warm[:], in_=warm[:])
-
-        ones = const.tile([P, GROUP_TILES * FEATURES], BF16)
-        nc.vector.memset(ones[:], 1.0)
 
         def spin_tensor(times):
             acc = acc_pool.tile([P, GROUP_TILES * FEATURES], F32)
@@ -248,7 +248,7 @@ def tile_lorentzmla_pb_t_kernel(tc, x, freqs_cos, freqs_sin, wq_w, wq_b, out):
         def live(n):
             return 0 <= n < N_GROUPS
 
-        for n in range(N_GROUPS + LEAD + 5):
+        for n in range(N_GROUPS + LEAD + 6):
             if live(n):
                 transpose_group(n)
                 regroup_group(n)
@@ -269,7 +269,7 @@ def tile_lorentzmla_pb_t_kernel(tc, x, freqs_cos, freqs_sin, wq_w, wq_b, out):
                 if 0 <= c < N_CHUNKS:
                     multiply_factors(c)
                     sum_products(c)
-            if live(n - LEAD - 3):
-                square_group(n - LEAD - 3)
-                if (n - LEAD - 3) % GROUPS_PER_CHUNK == GROUPS_PER_CHUNK - 1:
-                    finish_chunk((n - LEAD - 3) // GROUPS_PER_CHUNK)
+            if live(n - LEAD - 4):
+                square_group(n - LEAD - 4)
+                if (n - LEAD - 4) % GROUPS_PER_CHUNK == GROUPS_PER_CHUNK - 1:
+                    finish_chunk((n - LEAD - 4) // GROUPS_PER_CHUNK)

@@ -31,6 +31,7 @@ LOADS_AT_START = 16
 SPINS_AT_START = 3
 LEAD = 3
 W_AFTER = 1
+GPSIMD_TILES = 3
 
 FLOPS = 2 * BATCH * SEQ * K * FEATURES
 
@@ -206,13 +207,12 @@ def tile_lorentzmla_pb_t_kernel(tc, x, freqs_cos, freqs_sin, wq_w, wq_b, out):
             )
             rope_of[c] = products
 
-        def sum_products(c):
+        def sum_products(engine, c, tiles):
             halves = rope_of[c][:].rearrange("p (t h j e d) -> p t h j e d", t=CHUNK_TILES, h=HEADS, e=2, d=2)
-            engine = nc.vector if c == N_CHUNKS - 1 else nc.gpsimd
             engine.tensor_tensor(
-                out=rows_of(c)[:, :, :, 1 + NOPE : ROW].rearrange("p t h (j d) -> p t h j d", d=2),
-                in0=halves[:, :, :, :, 0],
-                in1=halves[:, :, :, :, 1],
+                out=rows_of(c)[:, tiles, :, 1 + NOPE : ROW].rearrange("p t h (j d) -> p t h j d", d=2),
+                in0=halves[:, tiles, :, :, 0],
+                in1=halves[:, tiles, :, :, 1],
                 op=ALU.add,
             )
 
@@ -263,12 +263,17 @@ def tile_lorentzmla_pb_t_kernel(tc, x, freqs_cos, freqs_sin, wq_w, wq_b, out):
                 if 0 <= c < N_CHUNKS:
                     for g in groups(c):
                         add_bias(g)
+                if 0 < c <= N_CHUNKS - 1:
+                    sum_products(nc.vector, c - 1, slice(GPSIMD_TILES, CHUNK_TILES))
                 for g in (n - 1, n):
                     if live(g):
                         quantise_group(g)
                 if 0 <= c < N_CHUNKS:
                     multiply_factors(c)
-                    sum_products(c)
+                    if c < N_CHUNKS - 1:
+                        sum_products(nc.gpsimd, c, slice(0, GPSIMD_TILES))
+                    else:
+                        sum_products(nc.vector, c, slice(0, CHUNK_TILES))
             if live(n - LEAD - 4):
                 square_group(n - LEAD - 4)
                 if (n - LEAD - 4) % GROUPS_PER_CHUNK == GROUPS_PER_CHUNK - 1:

@@ -29,6 +29,7 @@ GROUP_ROWS = GROUP_TILES * HEADS
 CHUNK_ROWS = CHUNK_TILES * HEADS
 LOADS_AT_START = 16
 SPINS_AT_START = 3
+HEAD_GROUPS = 5
 LEAD = 3
 W_AFTER = 1
 GPSIMD_TILES = 3
@@ -151,7 +152,7 @@ def tile_lorentzmla_pb_t_kernel(tc, x, freqs_cos, freqs_sin, wq_w, wq_b, out):
 
         def regroup_group(n):
             grouped = grouped_pool.tile([P, GROUP_TILES * K], BF16, align_bytes=64)
-            for t in range(GROUP_TILES):
+            for t in range(GROUP_TILES) if n < HEAD_GROUPS else reversed(range(GROUP_TILES)):
                 regroup(nc.scalar.copy, turned_of[n][t], grouped, t)
             grouped_of[n] = grouped
 
@@ -194,18 +195,20 @@ def tile_lorentzmla_pb_t_kernel(tc, x, freqs_cos, freqs_sin, wq_w, wq_b, out):
                 op=ALU.add,
             )
 
-        def multiply_factors(c):
-            products = rope_pool.tile([P, CHUNK_ROWS * PAIRS * 4], F32)
-            shape = [P, CHUNK_TILES, HEADS, 2 * PAIRS, 2]
+        def multiply_factors(c, tiles):
+            if c not in rope_of:
+                products = rope_pool.tile([P, CHUNK_ROWS * PAIRS * 4], F32)
+                rope_of[c] = products
+            shape = [P, tiles.stop - tiles.start, HEADS, 2 * PAIRS, 2]
             i0 = (c * CHUNK_TILES) % TOKENS_PER_PARTITION
             table = factors[:].rearrange("p (i o a d) -> p i o a d", o=1, a=2 * PAIRS, d=2)
+            rotary = rows_of(c)[:, tiles, :, 1 + NOPE : ROW]
             nc.vector.tensor_tensor(
-                out=products[:].rearrange("p (t h a d) -> p t h a d", t=CHUNK_TILES, h=HEADS, d=2),
-                in0=rows_of(c)[:, :, :, 1 + NOPE : ROW].rearrange("p t h (a o) -> p t h a o", o=1).to_broadcast(shape),
-                in1=table[:, i0 : i0 + CHUNK_TILES].to_broadcast(shape),
+                out=rope_of[c][:].rearrange("p (t h a d) -> p t h a d", t=CHUNK_TILES, h=HEADS, d=2)[:, tiles],
+                in0=rotary.rearrange("p t h (a o) -> p t h a o", o=1).to_broadcast(shape),
+                in1=table[:, i0 + tiles.start : i0 + tiles.stop].to_broadcast(shape),
                 op=ALU.mult,
             )
-            rope_of[c] = products
 
         def sum_products(engine, c, tiles):
             halves = rope_of[c][:].rearrange("p (t h j e d) -> p t h j e d", t=CHUNK_TILES, h=HEADS, e=2, d=2)
@@ -216,6 +219,8 @@ def tile_lorentzmla_pb_t_kernel(tc, x, freqs_cos, freqs_sin, wq_w, wq_b, out):
                 op=ALU.add,
             )
 
+        unused_by_vector = const.tile([P, GROUP_ROWS * HEAD], BF16)
+
         def square_group(n):
             c, part = divmod(n, GROUPS_PER_CHUNK)
             if part == 0:
@@ -225,9 +230,10 @@ def tile_lorentzmla_pb_t_kernel(tc, x, freqs_cos, freqs_sin, wq_w, wq_b, out):
             unused = rope_pool.tile([P, GROUP_ROWS * HEAD], BF16)
             for r in range(GROUP_ROWS):
                 row = rows[:, part * GROUP_ROWS + r, 1:ROW]
-                squares = unused[:, r * HEAD : (r + 1) * HEAD]
+                by_vector = n == N_GROUPS - 1 and r >= GROUP_ROWS // 2
+                squares = (unused_by_vector if by_vector else unused)[:, r * HEAD : (r + 1) * HEAD]
                 total = squares_of[c][:, part * GROUP_ROWS + r, :]
-                if n == N_GROUPS - 1:
+                if by_vector:
                     nc.vector.scalar_tensor_tensor(
                         out=squares, in0=row, scalar=1.0, in1=row, op0=ALU.mult, op1=ALU.mult, accum_out=total
                     )
@@ -248,10 +254,12 @@ def tile_lorentzmla_pb_t_kernel(tc, x, freqs_cos, freqs_sin, wq_w, wq_b, out):
         def live(n):
             return 0 <= n < N_GROUPS
 
-        for n in range(N_GROUPS + LEAD + 6):
+        for n in range(N_GROUPS + LEAD + 7):
             if live(n):
                 transpose_group(n)
                 regroup_group(n)
+            if live(n - LEAD - 5) and (n - LEAD - 5) % GROUPS_PER_CHUNK == GROUPS_PER_CHUNK - 1:
+                finish_chunk((n - LEAD - 5) // GROUPS_PER_CHUNK)
             if n == W_AFTER:
                 prepare_weights()
             if live(n - LEAD):
@@ -265,16 +273,17 @@ def tile_lorentzmla_pb_t_kernel(tc, x, freqs_cos, freqs_sin, wq_w, wq_b, out):
                         add_bias(g)
                 if 0 < c <= N_CHUNKS - 1:
                     sum_products(nc.vector, c - 1, slice(GPSIMD_TILES, CHUNK_TILES))
-                for g in (n - 1, n):
+                for g in (n - 1, n) if n < HEAD_GROUPS else (n, n - 1):
                     if live(g):
                         quantise_group(g)
                 if 0 <= c < N_CHUNKS:
-                    multiply_factors(c)
                     if c < N_CHUNKS - 1:
+                        multiply_factors(c, slice(0, CHUNK_TILES))
                         sum_products(nc.gpsimd, c, slice(0, GPSIMD_TILES))
                     else:
-                        sum_products(nc.vector, c, slice(0, CHUNK_TILES))
+                        for part in range(GROUPS_PER_CHUNK):
+                            multiply_factors(c, slice(part * GROUP_TILES, (part + 1) * GROUP_TILES))
+                        for part in range(GROUPS_PER_CHUNK):
+                            sum_products(nc.vector, c, slice(part * GROUP_TILES, (part + 1) * GROUP_TILES))
             if live(n - LEAD - 4):
                 square_group(n - LEAD - 4)
-                if (n - LEAD - 4) % GROUPS_PER_CHUNK == GROUPS_PER_CHUNK - 1:
-                    finish_chunk((n - LEAD - 4) // GROUPS_PER_CHUNK)

from contextlib import ExitStack

import concourse.mybir as mybir
from concourse.masks import make_identity

F32 = mybir.dt.float32
BF16 = mybir.dt.bfloat16
U32 = mybir.dt.uint32
U8 = mybir.dt.uint8
FP8X4 = mybir.dt.float8_e4m3fn_x4
ACT = mybir.ActivationFunctionType
ALU = mybir.AluOpType

P = 128
BATCH, SEQ, K = 8, 1024, 1024
HEADS, HEAD, NOPE, PAIRS = 2, 128, 64, 32
FEATURES = HEADS * HEAD
ROW = HEAD + 1
TOKENS_PER_PARTITION = SEQ // P
PASSES = K // 512
WORDS = K // 2
GROUP_TILES = 2
CHUNK_TILES = 4
GROUPS_PER_CHUNK = CHUNK_TILES // GROUP_TILES
CHUNKS_PER_BATCH = TOKENS_PER_PARTITION // CHUNK_TILES
N_CHUNKS = BATCH * CHUNKS_PER_BATCH
N_GROUPS = N_CHUNKS * GROUPS_PER_CHUNK
GROUP_ROWS = GROUP_TILES * HEADS
CHUNK_ROWS = CHUNK_TILES * HEADS
LOADS_AT_START = 16
SPINS_AT_START = 3
HEAD_GROUPS = 5
LEAD = 3
W_AFTER = 1
GPSIMD_TILES = 3

FLOPS = 2 * BATCH * SEQ * K * FEATURES


def tile_lorentzmla_pb_t_kernel(tc, x, freqs_cos, freqs_sin, wq_w, wq_b, out):
    nc = tc.nc
    with ExitStack() as stack:
        const = stack.enter_context(tc.tile_pool(name="const", bufs=1))
        x_pool = stack.enter_context(tc.tile_pool(name="x", bufs=N_GROUPS - 1))
        grouped_pool = stack.enter_context(tc.tile_pool(name="grouped", bufs=6))
        mx_pool = stack.enter_context(tc.tile_pool(name="mx", bufs=6))
        rope_pool = stack.enter_context(tc.tile_pool(name="rope", bufs=3))
        out_pool = stack.enter_context(tc.tile_pool(name="out", bufs=6))
        turned_pool = stack.enter_context(tc.psum_pool(name="turned", bufs=4))
        acc_pool = stack.enter_context(tc.psum_pool(name="acc", bufs=4))
        stack.enter_context(tc.manual_schedule())

        ones = const.tile([P, GROUP_TILES * FEATURES], BF16)
        nc.vector.memset(ones[:], 1.0)

        cos_sb = const.tile([P, TOKENS_PER_PARTITION * PAIRS], BF16)
        sin_sb = const.tile([P, TOKENS_PER_PARTITION * PAIRS], BF16)
        nc.scalar.dma_start(out=cos_sb[:], in_=freqs_cos.rearrange("(p i) j -> p (i j)", i=TOKENS_PER_PARTITION))
        nc.scalar.dma_start(out=sin_sb[:], in_=freqs_sin.rearrange("(p i) j -> p (i j)", i=TOKENS_PER_PARTITION))
        bias_row = const.tile([P, FEATURES], BF16)
        nc.vector.memset(bias_row[:], 1.0)
        nc.scalar.dma_start(out=bias_row[0:1, :], in_=wq_b.rearrange("(o f) -> o f", o=1))

        x_src = x.rearrange("b (p i) k -> b p (i k)", i=TOKENS_PER_PARTITION)
        x_tiles = {}

        def load_group(n):
            b, part = divmod(n, TOKENS_PER_PARTITION // GROUP_TILES)
            x_sb = x_pool.tile([P, GROUP_TILES * K], BF16)
            cols = slice(part * GROUP_TILES * K, (part + 1) * GROUP_TILES * K)
            nc.sync.dma_start(out=x_sb[:], in_=x_src[b][:, cols])
            for t in range(GROUP_TILES):
                x_tiles[(n, t)] = x_sb[:, t * K : (t + 1) * K]

        for t in range(GROUP_TILES):
            x_first = const.tile([P, K], BF16, name="x_first_%d" % t)
            nc.sync.dma_start(out=x_first[:], in_=x_src[0][:, t * K : (t + 1) * K])
            x_tiles[(0, t)] = x_first[:]

        w_sb = const.tile([P, HEADS * K], BF16)
        for n in range(1, LOADS_AT_START):
            load_group(n)
            if n == W_AFTER:
                nc.sync.dma_start(
                    out=w_sb[:].rearrange("f (h k) -> f h k", h=HEADS), in_=wq_w.rearrange("(h f) k -> f h k", h=HEADS)
                )

        ident = const.tile([P, P], F32)
        make_identity(nc, ident[:])

        warm = const.tile([P, 1], F32)
        nc.vector.memset(warm[:], 1.0)
        nc.scalar.sqrt(out=warm[:], in_=warm[:])

        def spin_tensor(times):
            acc = acc_pool.tile([P, GROUP_TILES * FEATURES], F32)
            for i in range(times):
                nc.tensor.matmul(out=acc[:], lhsT=ones[:, 0:P], rhs=ones[:], start=True, stop=True)

        spin_tensor(SPINS_AT_START)

        def transpose_rows(rows_bf16):
            words = rows_bf16.bitcast(F32)
            turned = turned_pool.tile([P, WORDS], F32)
            for block in range(WORDS // P):
                g, u = divmod(block, 2)
                nc.tensor.transpose(
                    turned[:, block * P : (block + 1) * P], words[:, 2 * P * g + u : 2 * P * (g + 1) : 2], ident[:]
                )
            return turned

        def regroup(copy, turned, grouped, t):
            dst = grouped[:].bitcast(F32).rearrange("p (g t r u) -> p g t r u", g=PASSES, t=GROUP_TILES, u=2)
            copy(out=dst[:, :, t], in_=turned[:].rearrange("p (g u r) -> p g r u", g=PASSES, u=2))

        def quantise(grouped, codes, scales):
            nc.vector.quantize_mx(out=codes[:].bitcast(FP8X4), scales=scales[:], in_=grouped[:])

        factors = const.tile([P, TOKENS_PER_PARTITION * PAIRS * 4], BF16)
        factor = factors[:].rearrange("p (q e d) -> p q e d", e=2, d=2)
        nc.vector.tensor_copy(out=factor[:, :, 0, 0], in_=cos_sb[:])
        nc.vector.tensor_copy(out=factor[:, :, 0, 1], in_=sin_sb[:])
        nc.vector.tensor_scalar_mul(out=factor[:, :, 1, 0], in0=sin_sb[:], scalar1=-1.0)
        nc.vector.tensor_copy(out=factor[:, :, 1, 1], in_=cos_sb[:])
        first = const.tile([P, 1], BF16)
        nc.vector.tensor_copy(out=first[:], in_=ident[:, 0:1])
        bias = const.tile([P, FEATURES], F32)
        bias_rows = bias[:].rearrange("p (o h f) -> p o h f", o=1, h=HEADS).to_broadcast([P, GROUP_TILES, HEADS, HEAD])

        w_grouped = const.tile([P, GROUP_TILES * K], BF16, align_bytes=64)
        w_codes = const.tile([P, PASSES * FEATURES], U32, align_bytes=64)
        w_scales = const.tile([P, PASSES * FEATURES], U8, align_bytes=64)

        def prepare_weights():
            for h in range(HEADS):
                w_turned = transpose_rows(w_sb[:, h * K : (h + 1) * K])
                regroup(nc.vector.tensor_copy, w_turned, w_grouped, h)
            quantise(w_grouped, w_codes, w_scales)
            acc = acc_pool.tile([P, GROUP_TILES * FEATURES], F32)
            nc.tensor.matmul(
                out=acc[:, 0:FEATURES], lhsT=first[:].to_broadcast([P, P]), rhs=bias_row[:], start=True, stop=True
            )
            nc.scalar.copy(out=bias[:], in_=acc[:, 0:FEATURES])

        turned_of, grouped_of, mx_of, acc_of, rope_of, out_of, squares_of = {}, {}, {}, {}, {}, {}, {}

        def groups(c):
            return range(c * GROUPS_PER_CHUNK, (c + 1) * GROUPS_PER_CHUNK)

        def transpose_group(n):
            turned_of[n] = [transpose_rows(x_tiles[(n, t)]) for t in range(GROUP_TILES)]

        def regroup_group(n):
            grouped = grouped_pool.tile([P, GROUP_TILES * K], BF16, align_bytes=64)
            for t in range(GROUP_TILES) if n < HEAD_GROUPS else reversed(range(GROUP_TILES)):
                regroup(nc.scalar.copy, turned_of[n][t], grouped, t)
            grouped_of[n] = grouped

        def quantise_group(n):
            codes = mx_pool.tile([P, PASSES * GROUP_TILES * P], U32, align_bytes=64)
            scales = mx_pool.tile([P, PASSES * GROUP_TILES * P], U8, align_bytes=64)
            quantise(grouped_of[n], codes, scales)
            mx_of[n] = (codes, scales)

        def multiply_group(n):
            codes, scales = mx_of[n]
            acc = acc_pool.tile([P, GROUP_TILES * FEATURES], F32)
            for t in range(GROUP_TILES):
                for g in range(PASSES):
                    tokens = slice((g * GROUP_TILES + t) * P, (g * GROUP_TILES + t + 1) * P)
                    feats = slice(g * FEATURES, (g + 1) * FEATURES)
                    nc.tensor.matmul_mx(
                        out=acc[:, t * FEATURES : (t + 1) * FEATURES],
                        lhsT=codes[:, tokens].bitcast(FP8X4),
                        lhsT_scale=scales[:, tokens],
                        rhs=w_codes[:, feats].bitcast(FP8X4),
                        rhs_scale=w_scales[:, feats],
                        start=(g == 0),
                        stop=(g == PASSES - 1),
                    )
            acc_of[n] = acc

        def rows_of(c):
            return out_of[c][:].rearrange("p (t h c) -> p t h c", h=HEADS, c=ROW)

        def add_bias(n):
            c, part = divmod(n, GROUPS_PER_CHUNK)
            if part == 0:
                out_sb = out_pool.tile([P, CHUNK_ROWS * ROW], F32)
                out_of[c] = out_sb
            nc.vector.tensor_tensor(
                out=rows_of(c)[:, part * GROUP_TILES : (part + 1) * GROUP_TILES, :, 1:ROW],
                in0=acc_of[n][:].rearrange("p (t h f) -> p t h f", t=GROUP_TILES, h=HEADS),
                in1=bias_rows,
                op=ALU.add,
            )

        def multiply_factors(c, tiles):
            if c not in rope_of:
                products = rope_pool.tile([P, CHUNK_ROWS * PAIRS * 4], F32)
                rope_of[c] = products
            shape = [P, tiles.stop - tiles.start, HEADS, 2 * PAIRS, 2]
            i0 = (c * CHUNK_TILES) % TOKENS_PER_PARTITION
            table = factors[:].rearrange("p (i o a d) -> p i o a d", o=1, a=2 * PAIRS, d=2)
            rotary = rows_of(c)[:, tiles, :, 1 + NOPE : ROW]
            nc.vector.tensor_tensor(
                out=rope_of[c][:].rearrange("p (t h a d) -> p t h a d", t=CHUNK_TILES, h=HEADS, d=2)[:, tiles],
                in0=rotary.rearrange("p t h (a o) -> p t h a o", o=1).to_broadcast(shape),
                in1=table[:, i0 + tiles.start : i0 + tiles.stop].to_broadcast(shape),
                op=ALU.mult,
            )

        def sum_products(engine, c, tiles):
            halves = rope_of[c][:].rearrange("p (t h j e d) -> p t h j e d", t=CHUNK_TILES, h=HEADS, e=2, d=2)
            engine.tensor_tensor(
                out=rows_of(c)[:, tiles, :, 1 + NOPE : ROW].rearrange("p t h (j d) -> p t h j d", d=2),
                in0=halves[:, tiles, :, :, 0],
                in1=halves[:, tiles, :, :, 1],
                op=ALU.add,
            )

        unused_by_vector = const.tile([P, GROUP_ROWS * HEAD], BF16)

        def square_group(n):
            c, part = divmod(n, GROUPS_PER_CHUNK)
            if part == 0:
                sums = out_pool.tile([P, CHUNK_ROWS, 1], F32)
                squares_of[c] = sums
            rows = out_of[c][:].rearrange("p (r c) -> p r c", c=ROW)
            unused = rope_pool.tile([P, GROUP_ROWS * HEAD], BF16)
            for r in range(GROUP_ROWS):
                row = rows[:, part * GROUP_ROWS + r, 1:ROW]
                by_vector = n == N_GROUPS - 1 and r >= GROUP_ROWS // 2
                squares = (unused_by_vector if by_vector else unused)[:, r * HEAD : (r + 1) * HEAD]
                total = squares_of[c][:, part * GROUP_ROWS + r, :]
                if by_vector:
                    nc.vector.scalar_tensor_tensor(
                        out=squares, in0=row, scalar=1.0, in1=row, op0=ALU.mult, op1=ALU.mult, accum_out=total
                    )
                else:
                    nc.scalar.activation(out=squares, in_=row, func=ACT.Square, accum_out=total)

        def finish_chunk(c):
            b, part = divmod(c, CHUNKS_PER_BATCH)
            rows = out_of[c][:].rearrange("p (r c) -> p r c", c=ROW)
            nc.scalar.activation(out=rows[:, :, 0:1], in_=squares_of[c][:], func=ACT.Sqrt, bias=1.0)
            dst = out[b].rearrange("(p i) h c -> p (i h c)", i=TOKENS_PER_PARTITION)
            cols = slice(part * CHUNK_ROWS * ROW, (part + 1) * CHUNK_ROWS * ROW)
            nc.sync.dma_start(out=dst[:, cols], in_=out_of[c][:])
            loaded = len(x_tiles) // GROUP_TILES
            for n in range(loaded, min(loaded + GROUPS_PER_CHUNK, N_GROUPS)):
                load_group(n)

        def live(n):
            return 0 <= n < N_GROUPS

        for n in range(N_GROUPS + LEAD + 7):
            if live(n):
                transpose_group(n)
                regroup_group(n)
            if live(n - LEAD - 5) and (n - LEAD - 5) % GROUPS_PER_CHUNK == GROUPS_PER_CHUNK - 1:
                finish_chunk((n - LEAD - 5) // GROUPS_PER_CHUNK)
            if n == W_AFTER:
                prepare_weights()
            if live(n - LEAD):
                multiply_group(n - LEAD)
            elif n < LEAD:
                spin_tensor(1)
            c, part = divmod(n - LEAD - 1, GROUPS_PER_CHUNK)
            if part == 0:
                if 0 <= c < N_CHUNKS:
                    for g in groups(c):
                        add_bias(g)
                if 0 < c <= N_CHUNKS - 1:
                    sum_products(nc.vector, c - 1, slice(GPSIMD_TILES, CHUNK_TILES))
                for g in (n - 1, n) if n < HEAD_GROUPS else (n, n - 1):
                    if live(g):
                        quantise_group(g)
                if 0 <= c < N_CHUNKS:
                    if c < N_CHUNKS - 1:
                        multiply_factors(c, slice(0, CHUNK_TILES))
                        sum_products(nc.gpsimd, c, slice(0, GPSIMD_TILES))
                    else:
                        for part in range(GROUPS_PER_CHUNK):
                            multiply_factors(c, slice(part * GROUP_TILES, (part + 1) * GROUP_TILES))
                        for part in range(GROUPS_PER_CHUNK):
                            sum_products(nc.vector, c, slice(part * GROUP_TILES, (part + 1) * GROUP_TILES))
            if live(n - LEAD - 4):
                square_group(n - LEAD - 4)
